import numpy as np
import ml_dtypes


def mxq(x, axis, fmt="e4m3"):
    dtype, down = {"e4m3": (ml_dtypes.float8_e4m3fn, 7), "e5m2": (ml_dtypes.float8_e5m2, 14)}[fmt]
    v = np.moveaxis(np.asarray(x, np.float32).astype(ml_dtypes.bfloat16).astype(np.float64), axis, -1)
    blocks = v.reshape(v.shape[:-1] + (-1, 32))
    amax = np.abs(blocks).max(-1, keepdims=True)
    byte = np.maximum(np.where(amax > 0, np.frexp(amax)[1] - 1 + 127, 0) - down, 1)
    scale = np.exp2(byte - 127.0)
    codes = (blocks / scale).astype(np.float32).astype(dtype).astype(np.float64)
    return np.moveaxis((codes * scale).reshape(v.shape), -1, axis)


WIDE = False


def mx_kscale(k):
    if not WIDE:
        return np.ones(k)
    levels = np.array([20, -20, 10, -10, 0])
    a = np.random.permutation(np.resize(levels, k // 512 * 4)).reshape(k // 512, 4)
    idx = np.arange(k)
    return np.exp2(a[idx // 512, idx % 128 // 32])


BF16 = ml_dtypes.bfloat16


def bf(x):
    return np.asarray(x, np.float32).astype(BF16)


def f64(x):
    return np.asarray(x).astype(np.float64)


B, N, D, R, Q = 4, 1024, 1024, 16, 16
T = B * N
K = R * Q + Q * R


def flat_core(c):
    return f64(c).transpose(1, 0, 2).reshape(D, -1)


def setup_inputs():
    a = np.repeat(mx_kscale(K)[0:R * Q:32], 2)
    x = bf(np.random.standard_normal((B, N, D)))
    w00 = bf(np.random.standard_normal((B, N, R)))
    c10 = bf(np.random.standard_normal((R, D, Q)) / np.sqrt(D * R))
    core2 = bf(np.random.standard_normal((Q, D, R)) / np.sqrt(D * Q))
    g = bf(np.random.standard_normal((B, N, R)) * np.exp2(np.random.randint(-12, 1, (B, N, 1))) * 64.0)
    xf = f64(x).reshape(T, D)
    m1 = (xf @ flat_core(c10)).reshape(B, N, R, Q)
    m2 = (xf @ flat_core(core2)).reshape(B, N, Q, R)
    w1 = (f64(w00)[..., :, None] * m1).sum(-2)
    return {"x": x,
            "w0": bf(f64(w00) * a),
            "core1": bf(f64(c10) / a[:, None, None]),
            "core2": core2,
            "w1": np.asarray(w1, np.float32),
            "m2": np.asarray(m2, np.float32),
            "grad_out": g}


def reference(x, w0, core1, core2, w1, m2, grad_out):
    g = f64(grad_out).reshape(T, R)
    m2f = f64(m2).reshape(T, Q, R)
    dw1 = (m2f * g[:, None, :]).sum(-1)
    dm1 = f64(w0).reshape(T, R)[:, :, None] * dw1[:, None, :]
    dm2 = f64(w1).reshape(T, Q)[:, :, None] * g[:, None, :]
    dm = np.concatenate([dm1.reshape(T, R * Q), dm2.reshape(T, Q * R)], axis=1)
    cc = np.concatenate([flat_core(core1), flat_core(core2)], axis=1)
    return (mxq(dm, 1, "e5m2") @ mxq(cc, 1, "e4m3").T).reshape(B, N, D)

@@ -1,0 +1,212 @@
+from contextlib import ExitStack
+
+import concourse.mybir as mybir
+from concourse.masks import make_identity
+
+F32 = mybir.dt.float32
+BF16 = mybir.dt.bfloat16
+U32 = mybir.dt.uint32
+U8 = mybir.dt.uint8
+E4M3_X4 = mybir.dt.float8_e4m3fn_x4
+E5M2_X4 = mybir.dt.float8_e5m2_x4
+MULT = mybir.AluOpType.mult
+ADD = mybir.AluOpType.add
+
+P = 128
+PACK = 4
+T = 4096
+D = 1024
+RANK = 16
+HALF_K = RANK * RANK
+K = 2 * HALF_K
+TILES = T // P
+BANK = 512
+TURNS = BANK // P
+D_BANKS = D // BANK
+D_PER_PART = D // P
+GROUP = 2
+ROUNDS = TILES // GROUP
+LOAD_TILES = 4
+VECTOR_EVERY = 8
+
+FLOPS = 2 * T * D * K
+BYTES = 4 * T * D + 4 * T * HALF_K + 4 * T * RANK + 2 * 2 * T * RANK + 2 * 2 * D * HALF_K
+
+
+def tile_linear_pa_v_kernel(tc, x, w0, core1, core2, w1, m2, grad_out, out):
+    nc = tc.nc
+    outer = [P, GROUP, RANK, RANK]
+
+    w0_dram = w0.flatten_outer_dims().rearrange("(p n) r -> p n r", n=TILES)
+    w1_dram = w1.flatten_outer_dims().rearrange("(p n) q -> p n q", n=TILES)
+    g_dram = grad_out.flatten_outer_dims().rearrange("(p n) r -> p n r", n=TILES)
+    m2_dram = m2.rearrange("b s q r -> (b s) (q r)").rearrange("(p n) f -> p n f", n=TILES)
+    out_dram = out.flatten_outer_dims().rearrange("(p n) d -> p n d", n=TILES)
+
+    with ExitStack() as ctx:
+        ctx.enter_context(tc.manual_schedule())
+        const = ctx.enter_context(tc.tile_pool(name="const", bufs=1))
+        short = ctx.enter_context(tc.tile_pool(name="short", bufs=2))
+        kept = ctx.enter_context(tc.tile_pool(name="kept", bufs=3))
+        out_pool = ctx.enter_context(tc.tile_pool(name="out", bufs=4))
+        turn_psum = ctx.enter_context(tc.psum_pool(name="turn", bufs=2))
+        acc_psum = ctx.enter_context(tc.psum_pool(name="acc", bufs=6))
+
+        ident = const.tile([P, P], F32)
+        make_identity(nc, ident[:])
+
+        cc_raw = const.tile([P, D_PER_PART * K], BF16)
+        for h, core in enumerate((core1, core2)):
+            nc.scalar.dma_start(
+                out=cc_raw[:, h * D_PER_PART * HALF_K : (h + 1) * D_PER_PART * HALF_K].rearrange(
+                    "p (a f) -> p a f", a=RANK
+                ),
+                in_=core.rearrange("a (p s) c -> p a (s c)", s=D_PER_PART),
+            )
+        g_sb = const.tile([P, TILES, RANK], BF16)
+        w0_sb = const.tile([P, TILES, RANK], BF16)
+        w1_sb = const.tile([P, TILES, RANK], F32)
+        m2_sb = [
+            const.tile([P, LOAD_TILES, HALF_K], F32, name="m2_%d" % c) for c in range(TILES // LOAD_TILES)
+        ]
+        nc.sync.dma_start(out=g_sb[:], in_=g_dram)
+        nc.sync.dma_start(out=m2_sb[0][:], in_=m2_dram[:, 0:LOAD_TILES, :])
+        nc.sync.dma_start(out=w1_sb[:], in_=w1_dram)
+        nc.sync.dma_start(out=w0_sb[:], in_=w0_dram)
+        for c in range(1, TILES // LOAD_TILES):
+            nc.sync.dma_start(out=m2_sb[c][:], in_=m2_dram[:, c * LOAD_TILES : (c + 1) * LOAD_TILES, :])
+
+        cc_rows = const.tile([P, D_PER_PART * K], BF16)
+        cc_grouped = const.tile([P, D * PACK], BF16, align_bytes=64)
+        cc_codes = const.tile([P, D], U32, align_bytes=64)
+        cc_scales = const.tile([P, D], U8, align_bytes=64)
+
+        def sort_cc():
+            pairs = RANK // 2
+            raw = cc_raw[:].bitcast(F32).rearrange("p (h a s c) -> p h s a c", h=2, a=RANK, c=pairs)
+            rows = cc_rows[:].bitcast(F32).rearrange("p (s h a c) -> p h s a c", h=2, a=RANK, c=pairs)
+            for h in range(2):
+                nc.scalar.copy(out=rows[:, h], in_=raw[:, h])
+
+        def turn_and_quantise_cc():
+            words = cc_rows[:].bitcast(F32).rearrange("p (s i u) -> p s i u", s=D_PER_PART, u=2)
+            banks = D_PER_PART * 2 // TURNS
+            grouped_words = cc_grouped[:].bitcast(F32).rearrange("p (c b f) -> p c b f", b=banks, f=TURNS)
+            for bank in range(banks):
+                turned_cc = acc_psum.tile([P, BANK], F32, tag="acc")
+                for f in range(TURNS):
+                    nc.tensor.transpose(
+                        turned_cc[:, f * P : (f + 1) * P], words[:, 2 * bank + f // 2, :, f % 2], ident[:]
+                    )
+                nc.scalar.copy(
+                    out=grouped_words[:, :, bank, :], in_=turned_cc[:].rearrange("p (f c) -> p c f", f=TURNS)
+                )
+            for b in range(D_BANKS):
+                cols = slice(b * BANK, (b + 1) * BANK)
+                nc.vector.quantize_mx(
+                    out=cc_codes[:, cols].bitcast(E4M3_X4),
+                    scales=cc_scales[:, cols],
+                    in_=cc_grouped[:, b * BANK * PACK : (b + 1) * BANK * PACK],
+                )
+
+        dm_of = {}
+        dw1_of = {}
+        grouped_of = {}
+        packed_of = {}
+
+        def start_dm(rnd):
+            tiles = slice(rnd * GROUP, (rnd + 1) * GROUP)
+            first = rnd * GROUP % LOAD_TILES
+            m2_rnd = m2_sb[rnd * GROUP // LOAD_TILES][:, first : first + GROUP, :]
+            g_rnd = g_sb[:, tiles, :].unsqueeze(2).to_broadcast(outer)
+            prod = short.tile(outer, F32)
+            nc.vector.tensor_tensor(
+                out=prod[:], in0=m2_rnd.rearrange("p n (q r) -> p n q r", r=RANK), in1=g_rnd, op=MULT
+            )
+            dm = kept.tile([P, GROUP * K], BF16)
+            nc.vector.tensor_tensor(
+                out=dm[:].rearrange("p (n h a c) -> p h n a c", h=2, a=RANK, c=RANK)[:, 1],
+                in0=w1_sb[:, tiles, :].unsqueeze(3).to_broadcast(outer),
+                in1=g_rnd,
+                op=MULT,
+            )
+            dw1 = short.tile([P, GROUP, RANK], F32)
+            nc.vector.tensor_reduce(out=dw1[:], in_=prod[:], axis=mybir.AxisListType.X, op=ADD)
+            dm_of[rnd] = dm
+            dw1_of[rnd] = dw1
+
+        def finish_dm(rnd):
+            tiles = slice(rnd * GROUP, (rnd + 1) * GROUP)
+            nc.vector.tensor_tensor(
+                out=dm_of[rnd][:].rearrange("p (n h a c) -> p h n a c", h=2, a=RANK, c=RANK)[:, 0],
+                in0=w0_sb[:, tiles, :].unsqueeze(3).to_broadcast(outer),
+                in1=dw1_of[rnd][:].unsqueeze(2).to_broadcast(outer),
+                op=MULT,
+            )
+
+        def turn_dm(rnd):
+            words = dm_of[rnd][:].bitcast(F32).rearrange("p (n i u) -> p n i u", n=GROUP, u=2)
+            grouped = short.tile([P, GROUP * P * PACK], BF16, align_bytes=64)
+            grouped_words = grouped[:].bitcast(F32).rearrange("p (n c u) -> p n c u", n=GROUP, u=2)
+            for pair in range(GROUP // 2):
+                turned = turn_psum.tile([P, BANK], F32)
+                for f in range(TURNS):
+                    nc.tensor.transpose(
+                        turned[:, f * P : (f + 1) * P], words[:, 2 * pair + f // 2, :, f % 2], ident[:]
+                    )
+                nc.scalar.copy(
+                    out=grouped_words[:, 2 * pair : 2 * pair + 2],
+                    in_=turned[:].rearrange("p (n u c) -> p n c u", n=2, u=2),
+                )
+            grouped_of[rnd] = grouped
+
+        def quantise_dm(rnd):
+            dm_codes = kept.tile([P, GROUP * P], U32, align_bytes=64)
+            dm_scales = kept.tile([P, GROUP * P], U8, align_bytes=64)
+            nc.vector.quantize_mx(
+                out=dm_codes[:].bitcast(E5M2_X4), scales=dm_scales[:], in_=grouped_of[rnd][:]
+            )
+            packed_of[rnd] = (dm_codes, dm_scales)
+
+        def prepare(rnd):
+            if rnd < ROUNDS:
+                turn_dm(rnd)
+            if rnd + 1 < ROUNDS:
+                start_dm(rnd + 1)
+            if rnd < ROUNDS:
+                quantise_dm(rnd)
+            if rnd + 1 < ROUNDS:
+                finish_dm(rnd + 1)
+
+        def multiply_and_store(rnd):
+            dm_codes, dm_scales = packed_of[rnd]
+            out_sb = out_pool.tile([P, GROUP, D], F32)
+            for n in range(GROUP):
+                tokens = slice(n * P, (n + 1) * P)
+                for b in range(D_BANKS):
+                    cols = slice(b * BANK, (b + 1) * BANK)
+                    acc = acc_psum.tile([P, BANK], F32)
+                    nc.tensor.matmul_mx(
+                        out=acc[:],
+                        lhsT=dm_codes[:, tokens].bitcast(E5M2_X4),
+                        lhsT_scale=dm_scales[:, tokens],
+                        rhs=cc_codes[:, cols].bitcast(E4M3_X4),
+                        rhs_scale=cc_scales[:, cols],
+                        start=True,
+                        stop=True,
+                    )
+                    number = (rnd * GROUP + n) * D_BANKS + b
+                    if number % VECTOR_EVERY == VECTOR_EVERY - 1:
+                        nc.vector.tensor_copy(out=out_sb[:, n, cols], in_=acc[:])
+                    else:
+                        nc.scalar.copy(out=out_sb[:, n, cols], in_=acc[:])
+            nc.sync.dma_start(out=out_dram[:, rnd * GROUP : (rnd + 1) * GROUP, :], in_=out_sb[:])
+
+        start_dm(0)
+        sort_cc()
+        finish_dm(0)
+        prepare(0)
+        turn_and_quantise_cc()
+        for rnd in range(ROUNDS):
+            prepare(rnd + 1)
+            multiply_and_store(rnd)

@@ -27,7 +27,8 @@ D_PER_PART = D // P
 GROUP = 2
 ROUNDS = TILES // GROUP
 LOAD_TILES = 4
-VECTOR_EVERY = 8
+VECTOR_EVERY = 16
+LEAD = 3
 
 FLOPS = 2 * T * D * K
 BYTES = 4 * T * D + 4 * T * HALF_K + 4 * T * RANK + 2 * 2 * T * RANK + 2 * 2 * D * HALF_K
@@ -48,7 +49,7 @@ def tile_linear_pa_v_kernel(tc, x, w0, core1, core2, w1, m2, grad_out, out):
         const = ctx.enter_context(tc.tile_pool(name="const", bufs=1))
         short = ctx.enter_context(tc.tile_pool(name="short", bufs=2))
         kept = ctx.enter_context(tc.tile_pool(name="kept", bufs=3))
-        out_pool = ctx.enter_context(tc.tile_pool(name="out", bufs=4))
+        out_pool = ctx.enter_context(tc.tile_pool(name="out", bufs=8))
         turn_psum = ctx.enter_context(tc.psum_pool(name="turn", bufs=2))
         acc_psum = ctx.enter_context(tc.psum_pool(name="acc", bufs=6))
 
@@ -88,7 +89,7 @@ def tile_linear_pa_v_kernel(tc, x, w0, core1, core2, w1, m2, grad_out, out):
             for h in range(2):
                 nc.scalar.copy(out=rows[:, h], in_=raw[:, h])
 
-        def turn_and_quantise_cc():
+        def turn_cc():
             words = cc_rows[:].bitcast(F32).rearrange("p (s i u) -> p s i u", s=D_PER_PART, u=2)
             banks = D_PER_PART * 2 // TURNS
             grouped_words = cc_grouped[:].bitcast(F32).rearrange("p (c b f) -> p c b f", b=banks, f=TURNS)
@@ -101,6 +102,8 @@ def tile_linear_pa_v_kernel(tc, x, w0, core1, core2, w1, m2, grad_out, out):
                 nc.scalar.copy(
                     out=grouped_words[:, :, bank, :], in_=turned_cc[:].rearrange("p (f c) -> p c f", f=TURNS)
                 )
+
+        def quantise_cc():
             for b in range(D_BANKS):
                 cols = slice(b * BANK, (b + 1) * BANK)
                 nc.vector.quantize_mx(
@@ -172,17 +175,18 @@ def tile_linear_pa_v_kernel(tc, x, w0, core1, core2, w1, m2, grad_out, out):
             if rnd < ROUNDS:
                 turn_dm(rnd)
             if rnd + 1 < ROUNDS:
-                start_dm(rnd + 1)
+                finish_dm(rnd + 1)
+            if rnd + 2 < ROUNDS:
+                start_dm(rnd + 2)
             if rnd < ROUNDS:
                 quantise_dm(rnd)
-            if rnd + 1 < ROUNDS:
-                finish_dm(rnd + 1)
 
         def multiply_and_store(rnd):
             dm_codes, dm_scales = packed_of[rnd]
-            out_sb = out_pool.tile([P, GROUP, D], F32)
+            every = VECTOR_EVERY if rnd + LEAD < ROUNDS else 2
             for n in range(GROUP):
                 tokens = slice(n * P, (n + 1) * P)
+                out_sb = out_pool.tile([P, D], F32)
                 for b in range(D_BANKS):
                     cols = slice(b * BANK, (b + 1) * BANK)
                     acc = acc_psum.tile([P, BANK], F32)
@@ -196,17 +200,22 @@ def tile_linear_pa_v_kernel(tc, x, w0, core1, core2, w1, m2, grad_out, out):
                         stop=True,
                     )
                     number = (rnd * GROUP + n) * D_BANKS + b
-                    if number % VECTOR_EVERY == VECTOR_EVERY - 1:
-                        nc.vector.tensor_copy(out=out_sb[:, n, cols], in_=acc[:])
+                    if number % every == every - 1:
+                        nc.vector.tensor_copy(out=out_sb[:, cols], in_=acc[:])
                     else:
-                        nc.scalar.copy(out=out_sb[:, n, cols], in_=acc[:])
-            nc.sync.dma_start(out=out_dram[:, rnd * GROUP : (rnd + 1) * GROUP, :], in_=out_sb[:])
+                        nc.scalar.copy(out=out_sb[:, cols], in_=acc[:])
+                nc.sync.dma_start(out=out_dram[:, rnd * GROUP + n, :], in_=out_sb[:])
 
         start_dm(0)
         sort_cc()
         finish_dm(0)
-        prepare(0)
-        turn_and_quantise_cc()
+        turn_cc()
+        start_dm(1)
+        turn_dm(0)
+        finish_dm(1)
+        quantise_dm(0)
+        quantise_cc()
+        start_dm(2)
         for rnd in range(ROUNDS):
             prepare(rnd + 1)
             multiply_and_store(rnd)

@@ -45,7 +45,6 @@ def tile_linear_pa_v_kernel(tc, x, w0, core1, core2, w1, m2, grad_out, out):
     out_dram = out.flatten_outer_dims().rearrange("(p n) d -> p n d", n=TILES)
 
     with ExitStack() as ctx:
-        ctx.enter_context(tc.manual_schedule())
         const = ctx.enter_context(tc.tile_pool(name="const", bufs=1))
         short = ctx.enter_context(tc.tile_pool(name="short", bufs=2))
         kept = ctx.enter_context(tc.tile_pool(name="kept", bufs=3))

@@ -27,7 +27,7 @@ D_PER_PART = D // P
 GROUP = 2
 ROUNDS = TILES // GROUP
 LOAD_TILES = 4
-VECTOR_EVERY = 16
+VECTOR_EVERY = 6
 LEAD = 3
 
 FLOPS = 2 * T * D * K
@@ -48,12 +48,16 @@ def tile_linear_pa_v_kernel(tc, x, w0, core1, core2, w1, m2, grad_out, out):
         const = ctx.enter_context(tc.tile_pool(name="const", bufs=1))
         short = ctx.enter_context(tc.tile_pool(name="short", bufs=2))
         kept = ctx.enter_context(tc.tile_pool(name="kept", bufs=3))
+        ahead = ctx.enter_context(tc.tile_pool(name="ahead", bufs=6))
         out_pool = ctx.enter_context(tc.tile_pool(name="out", bufs=8))
         turn_psum = ctx.enter_context(tc.psum_pool(name="turn", bufs=2))
-        acc_psum = ctx.enter_context(tc.psum_pool(name="acc", bufs=6))
+        acc_psum = ctx.enter_context(tc.psum_pool(name="acc", bufs=5))
+        token_psum = ctx.enter_context(tc.psum_pool(name="token", bufs=1))
 
         ident = const.tile([P, P], F32)
         make_identity(nc, ident[:])
+        ident_bf16 = const.tile([P, P], BF16)
+        make_identity(nc, ident_bf16[:])
 
         cc_raw = const.tile([P, D_PER_PART * K], BF16)
         for h, core in enumerate((core1, core2)):
@@ -75,6 +79,16 @@ def tile_linear_pa_v_kernel(tc, x, w0, core1, core2, w1, m2, grad_out, out):
         nc.sync.dma_start(out=w0_sb[:], in_=w0_dram)
         for c in range(1, TILES // LOAD_TILES):
             nc.sync.dma_start(out=m2_sb[c][:], in_=m2_dram[:, c * LOAD_TILES : (c + 1) * LOAD_TILES, :])
+
+        in_psum = token_psum.tile([P, 2, TILES, RANK], BF16)
+        for slot, small in enumerate((g_sb, w0_sb)):
+            nc.tensor.matmul(
+                in_psum[:, slot].rearrange("p n r -> p (n r)"),
+                lhsT=ident_bf16[:],
+                rhs=small[:].rearrange("p n r -> p (n r)"),
+                start=True,
+                stop=True,
+            )
 
         cc_rows = const.tile([P, D_PER_PART * K], BF16)
         cc_grouped = const.tile([P, D * PACK], BF16, align_bytes=64)
@@ -120,16 +134,16 @@ def tile_linear_pa_v_kernel(tc, x, w0, core1, core2, w1, m2, grad_out, out):
             tiles = slice(rnd * GROUP, (rnd + 1) * GROUP)
             first = rnd * GROUP % LOAD_TILES
             m2_rnd = m2_sb[rnd * GROUP // LOAD_TILES][:, first : first + GROUP, :]
-            g_rnd = g_sb[:, tiles, :].unsqueeze(2).to_broadcast(outer)
+            g_rnd = in_psum[:, 0, tiles, :].unsqueeze(2).to_broadcast(outer)
             prod = short.tile(outer, F32)
             nc.vector.tensor_tensor(
                 out=prod[:], in0=m2_rnd.rearrange("p n (q r) -> p n q r", r=RANK), in1=g_rnd, op=MULT
             )
-            dm = kept.tile([P, GROUP * K], BF16)
-            nc.vector.tensor_tensor(
+            dm = ahead.tile([P, GROUP * K], BF16)
+            nc.gpsimd.tensor_tensor(
                 out=dm[:].rearrange("p (n h a c) -> p h n a c", h=2, a=RANK, c=RANK)[:, 1],
                 in0=w1_sb[:, tiles, :].unsqueeze(3).to_broadcast(outer),
-                in1=g_rnd,
+                in1=g_sb[:, tiles, :].unsqueeze(2).to_broadcast(outer),
                 op=MULT,
             )
             dw1 = short.tile([P, GROUP, RANK], F32)
@@ -141,7 +155,7 @@ def tile_linear_pa_v_kernel(tc, x, w0, core1, core2, w1, m2, grad_out, out):
             tiles = slice(rnd * GROUP, (rnd + 1) * GROUP)
             nc.vector.tensor_tensor(
                 out=dm_of[rnd][:].rearrange("p (n h a c) -> p h n a c", h=2, a=RANK, c=RANK)[:, 0],
-                in0=w0_sb[:, tiles, :].unsqueeze(3).to_broadcast(outer),
+                in0=in_psum[:, 1, tiles, :].unsqueeze(3).to_broadcast(outer),
                 in1=dw1_of[rnd][:].unsqueeze(2).to_broadcast(outer),
                 op=MULT,
             )

@@ -28,6 +28,9 @@ GROUP = 2
 ROUNDS = TILES // GROUP
 LOAD_TILES = 4
 VECTOR_EVERY = 6
+GPSIMD_ROUNDS = [r for r in range(2, ROUNDS) if r % 4 != 3]
+AHEAD = 4
+TAIL = 2
 LEAD = 3
 
 FLOPS = 2 * T * D * K
@@ -59,27 +62,34 @@ def tile_linear_pa_v_kernel(tc, x, w0, core1, core2, w1, m2, grad_out, out):
         ident_bf16 = const.tile([P, P], BF16)
         make_identity(nc, ident_bf16[:])
 
+        g_sb = const.tile([P, TILES, RANK], BF16)
+        w0_sb = const.tile([P, TILES, RANK], BF16)
+        w1_sb = const.tile([P, TILES, RANK], F32)
+        m2_of = {}
+
+        def load_m2(first, count):
+            m2_sb = const.tile([P, count, HALF_K], F32, name="m2_%d" % first)
+            nc.sync.dma_start(out=m2_sb[:], in_=m2_dram[:, first : first + count, :])
+            for n in range(count):
+                m2_of[first + n] = (m2_sb, n)
+
+        nc.sync.dma_start(out=g_sb[:], in_=g_dram)
+        nc.sync.dma_start(out=w1_sb[:], in_=w1_dram)
+        load_m2(0, GROUP)
+        nc.sync.dma_start(out=w0_sb[:], in_=w0_dram)
         cc_raw = const.tile([P, D_PER_PART * K], BF16)
         for h, core in enumerate((core1, core2)):
-            nc.scalar.dma_start(
+            nc.sync.dma_start(
                 out=cc_raw[:, h * D_PER_PART * HALF_K : (h + 1) * D_PER_PART * HALF_K].rearrange(
                     "p (a f) -> p a f", a=RANK
                 ),
                 in_=core.rearrange("a (p s) c -> p a (s c)", s=D_PER_PART),
             )
-        g_sb = const.tile([P, TILES, RANK], BF16)
-        w0_sb = const.tile([P, TILES, RANK], BF16)
-        w1_sb = const.tile([P, TILES, RANK], F32)
-        m2_sb = [
-            const.tile([P, LOAD_TILES, HALF_K], F32, name="m2_%d" % c) for c in range(TILES // LOAD_TILES)
-        ]
-        nc.sync.dma_start(out=g_sb[:], in_=g_dram)
-        nc.sync.dma_start(out=m2_sb[0][:], in_=m2_dram[:, 0:LOAD_TILES, :])
-        nc.sync.dma_start(out=w1_sb[:], in_=w1_dram)
-        nc.sync.dma_start(out=w0_sb[:], in_=w0_dram)
-        for c in range(1, TILES // LOAD_TILES):
-            nc.sync.dma_start(out=m2_sb[c][:], in_=m2_dram[:, c * LOAD_TILES : (c + 1) * LOAD_TILES, :])
+        load_m2(GROUP, LOAD_TILES - GROUP)
+        for first in range(LOAD_TILES, TILES, LOAD_TILES):
+            load_m2(first, LOAD_TILES)
 
+        ctx.enter_context(tc.manual_schedule(engines={mybir.EngineType.PE, mybir.EngineType.DVE, mybir.EngineType.Activation, mybir.EngineType.Pool}))
         in_psum = token_psum.tile([P, 2, TILES, RANK], BF16)
         for slot, small in enumerate((g_sb, w0_sb)):
             nc.tensor.matmul(
@@ -99,8 +109,8 @@ def tile_linear_pa_v_kernel(tc, x, w0, core1, core2, w1, m2, grad_out, out):
             pairs = RANK // 2
             raw = cc_raw[:].bitcast(F32).rearrange("p (h a s c) -> p h s a c", h=2, a=RANK, c=pairs)
             rows = cc_rows[:].bitcast(F32).rearrange("p (s h a c) -> p h s a c", h=2, a=RANK, c=pairs)
-            for h in range(2):
-                nc.scalar.copy(out=rows[:, h], in_=raw[:, h])
+            nc.scalar.copy(out=rows[:, 0], in_=raw[:, 0])
+            nc.vector.tensor_copy(out=rows[:, 1], in_=raw[:, 1])
 
         def turn_cc():
             words = cc_rows[:].bitcast(F32).rearrange("p (s i u) -> p s i u", s=D_PER_PART, u=2)
@@ -112,68 +122,90 @@ def tile_linear_pa_v_kernel(tc, x, w0, core1, core2, w1, m2, grad_out, out):
                     nc.tensor.transpose(
                         turned_cc[:, f * P : (f + 1) * P], words[:, 2 * bank + f // 2, :, f % 2], ident[:]
                     )
-                nc.scalar.copy(
-                    out=grouped_words[:, :, bank, :], in_=turned_cc[:].rearrange("p (f c) -> p c f", f=TURNS)
-                )
+                copy = nc.vector.tensor_copy if bank % 2 else nc.scalar.copy
+                copy(out=grouped_words[:, :, bank, :], in_=turned_cc[:].rearrange("p (f c) -> p c f", f=TURNS))
 
-        def quantise_cc():
-            for b in range(D_BANKS):
-                cols = slice(b * BANK, (b + 1) * BANK)
-                nc.vector.quantize_mx(
-                    out=cc_codes[:, cols].bitcast(E4M3_X4),
-                    scales=cc_scales[:, cols],
-                    in_=cc_grouped[:, b * BANK * PACK : (b + 1) * BANK * PACK],
-                )
+        def quantise_cc(b):
+            cols = slice(b * BANK, (b + 1) * BANK)
+            nc.vector.quantize_mx(
+                out=cc_codes[:, cols].bitcast(E4M3_X4),
+                scales=cc_scales[:, cols],
+                in_=cc_grouped[:, b * BANK * PACK : (b + 1) * BANK * PACK],
+            )
 
         dm_of = {}
         dw1_of = {}
         grouped_of = {}
         packed_of = {}
 
-        def start_dm(rnd):
+        prod_of = {}
+
+        def dm_tile(rnd):
+            if rnd not in dm_of:
+                dm_of[rnd] = ahead.tile([P, GROUP * K], BF16, name="dm")
+            return dm_of[rnd]
+
+        def second_half(rnd):
+            dm = dm_tile(rnd)
+            for n in range(GROUP):
+                tile = rnd * GROUP + n
+                nc.gpsimd.tensor_tensor(
+                    out=dm[:, n * K + HALF_K : (n + 1) * K].rearrange("p (a c) -> p a c", a=RANK),
+                    in0=w1_sb[:, tile, :].unsqueeze(2).to_broadcast([P, RANK, RANK]),
+                    in1=g_sb[:, tile, :].unsqueeze(1).to_broadcast([P, RANK, RANK]),
+                    op=MULT,
+                )
+
+        def products(rnd):
             tiles = slice(rnd * GROUP, (rnd + 1) * GROUP)
-            first = rnd * GROUP % LOAD_TILES
-            m2_rnd = m2_sb[rnd * GROUP // LOAD_TILES][:, first : first + GROUP, :]
-            g_rnd = in_psum[:, 0, tiles, :].unsqueeze(2).to_broadcast(outer)
-            prod = short.tile(outer, F32)
-            nc.vector.tensor_tensor(
-                out=prod[:], in0=m2_rnd.rearrange("p n (q r) -> p n q r", r=RANK), in1=g_rnd, op=MULT
-            )
-            dm = ahead.tile([P, GROUP * K], BF16)
-            nc.gpsimd.tensor_tensor(
-                out=dm[:].rearrange("p (n h a c) -> p h n a c", h=2, a=RANK, c=RANK)[:, 1],
-                in0=w1_sb[:, tiles, :].unsqueeze(3).to_broadcast(outer),
-                in1=g_sb[:, tiles, :].unsqueeze(2).to_broadcast(outer),
-                op=MULT,
-            )
-            dw1 = short.tile([P, GROUP, RANK], F32)
-            nc.vector.tensor_reduce(out=dw1[:], in_=prod[:], axis=mybir.AxisListType.X, op=ADD)
-            dm_of[rnd] = dm
+            m2_sb, first = m2_of[rnd * GROUP]
+            prod = ahead.tile(outer, F32)
+            if rnd in GPSIMD_ROUNDS:
+                for n in range(GROUP):
+                    nc.gpsimd.tensor_tensor(
+                        out=prod[:, n],
+                        in0=m2_sb[:, first + n, :].rearrange("p (q r) -> p q r", r=RANK),
+                        in1=g_sb[:, rnd * GROUP + n, :].unsqueeze(1).to_broadcast([P, RANK, RANK]),
+                        op=MULT,
+                    )
+            else:
+                nc.vector.tensor_tensor(
+                    out=prod[:],
+                    in0=m2_sb[:, first : first + GROUP, :].rearrange("p n (q r) -> p n q r", r=RANK),
+                    in1=in_psum[:, 0, tiles, :].unsqueeze(2).to_broadcast(outer),
+                    op=MULT,
+                )
+            prod_of[rnd] = prod
+
+        def sums(rnd):
+            dw1 = kept.tile([P, GROUP, RANK], F32)
+            nc.vector.tensor_reduce(out=dw1[:], in_=prod_of[rnd][:], axis=mybir.AxisListType.X, op=ADD)
             dw1_of[rnd] = dw1
 
         def finish_dm(rnd):
             tiles = slice(rnd * GROUP, (rnd + 1) * GROUP)
             nc.vector.tensor_tensor(
-                out=dm_of[rnd][:].rearrange("p (n h a c) -> p h n a c", h=2, a=RANK, c=RANK)[:, 0],
+                out=dm_tile(rnd)[:].rearrange("p (n h a c) -> p h n a c", h=2, a=RANK, c=RANK)[:, 0],
                 in0=in_psum[:, 1, tiles, :].unsqueeze(3).to_broadcast(outer),
                 in1=dw1_of[rnd][:].unsqueeze(2).to_broadcast(outer),
                 op=MULT,
             )
 
+        turned_of = {}
+
         def turn_dm(rnd):
             words = dm_of[rnd][:].bitcast(F32).rearrange("p (n i u) -> p n i u", n=GROUP, u=2)
-            grouped = short.tile([P, GROUP * P * PACK], BF16, align_bytes=64)
-            grouped_words = grouped[:].bitcast(F32).rearrange("p (n c u) -> p n c u", n=GROUP, u=2)
-            for pair in range(GROUP // 2):
-                turned = turn_psum.tile([P, BANK], F32)
-                for f in range(TURNS):
-                    nc.tensor.transpose(
-                        turned[:, f * P : (f + 1) * P], words[:, 2 * pair + f // 2, :, f % 2], ident[:]
-                    )
-                nc.scalar.copy(
-                    out=grouped_words[:, 2 * pair : 2 * pair + 2],
-                    in_=turned[:].rearrange("p (n u c) -> p n c u", n=2, u=2),
-                )
+            turned = turn_psum.tile([P, BANK], F32)
+            for f in range(TURNS):
+                nc.tensor.transpose(turned[:, f * P : (f + 1) * P], words[:, f // 2, :, f % 2], ident[:])
+            turned_of[rnd] = turned
+
+        def group_dm(rnd):
+            grouped = kept.tile([P, GROUP * P * PACK], BF16, align_bytes=64)
+            nc.scalar.copy(
+                out=grouped[:].bitcast(F32).rearrange("p (n c u) -> p n c u", n=GROUP, u=2),
+                in_=turned_of[rnd][:].rearrange("p (n u c) -> p n c u", n=GROUP, u=2),
+            )
             grouped_of[rnd] = grouped
 
         def quantise_dm(rnd):
@@ -184,22 +216,13 @@ def tile_linear_pa_v_kernel(tc, x, w0, core1, core2, w1, m2, grad_out, out):
             )
             packed_of[rnd] = (dm_codes, dm_scales)
 
-        def prepare(rnd):
-            if rnd < ROUNDS:
-                turn_dm(rnd)
-            if rnd + 1 < ROUNDS:
-                finish_dm(rnd + 1)
-            if rnd + 2 < ROUNDS:
-                start_dm(rnd + 2)
-            if rnd < ROUNDS:
-                quantise_dm(rnd)
+        acc_of = {}
+        out_of = {}
 
-        def multiply_and_store(rnd):
+        def multiply(rnd):
             dm_codes, dm_scales = packed_of[rnd]
-            every = VECTOR_EVERY if rnd + LEAD < ROUNDS else 2
             for n in range(GROUP):
                 tokens = slice(n * P, (n + 1) * P)
-                out_sb = out_pool.tile([P, D], F32)
                 for b in range(D_BANKS):
                     cols = slice(b * BANK, (b + 1) * BANK)
                     acc = acc_psum.tile([P, BANK], F32)
@@ -212,23 +235,53 @@ def tile_linear_pa_v_kernel(tc, x, w0, core1, core2, w1, m2, grad_out, out):
                         start=True,
                         stop=True,
                     )
-                    number = (rnd * GROUP + n) * D_BANKS + b
-                    if number % every == every - 1:
-                        nc.vector.tensor_copy(out=out_sb[:, cols], in_=acc[:])
-                    else:
-                        nc.scalar.copy(out=out_sb[:, cols], in_=acc[:])
-                nc.sync.dma_start(out=out_dram[:, rnd * GROUP + n, :], in_=out_sb[:])
+                    acc_of[rnd, n, b] = acc
 
-        start_dm(0)
-        sort_cc()
+        def empty(rnd, n, b, copy):
+            if b == 0:
+                out_of[rnd, n] = out_pool.tile([P, D], F32, name="out_sb")
+            copy(out=out_of[rnd, n][:, b * BANK : (b + 1) * BANK], in_=acc_of[rnd, n, b][:])
+            if b == 1:
+                nc.sync.dma_start(out=out_dram[:, rnd * GROUP + n, :], in_=out_of[rnd, n][:])
+
+        def for_round(step, rnd):
+            if rnd < ROUNDS:
+                step(rnd)
+
+        scalar, vector = nc.scalar.copy, nc.vector.tensor_copy
+
+        for rnd in range(3):
+            second_half(rnd)
+        products(0)
+        sums(0)
         finish_dm(0)
+        sort_cc()
+        products(1)
         turn_cc()
-        start_dm(1)
         turn_dm(0)
-        finish_dm(1)
+        group_dm(0)
+        sums(1)
+        quantise_cc(0)
         quantise_dm(0)
-        quantise_cc()
-        start_dm(2)
+        quantise_cc(1)
+        finish_dm(1)
+        products(2)
+        second_half(3)
+        products(3)
         for rnd in range(ROUNDS):
-            prepare(rnd + 1)
-            multiply_and_store(rnd)
+            if rnd:
+                quantise_dm(rnd)
+            if rnd:
+                for_round(turn_dm, rnd + 1)
+            multiply(rnd)
+            if not rnd:
+                for_round(turn_dm, rnd + 1)
+            for_round(products, rnd + AHEAD)
+            for_round(second_half, rnd + AHEAD)
+            empty(rnd, 0, 0, scalar)
+            for_round(group_dm, rnd + 1)
+            for_round(sums, rnd + 2)
+            empty(rnd, 0, 1, scalar)
+            for_round(finish_dm, rnd + 2)
+            empty(rnd, 1, 0, vector if rnd >= ROUNDS - TAIL else scalar)
+            empty(rnd, 1, 1, vector if (rnd + AHEAD >= ROUNDS or rnd + AHEAD in GPSIMD_ROUNDS) else scalar)

@@ -23,15 +23,11 @@ TILES = T // P
 BANK = 512
 TURNS = BANK // P
 D_BANKS = D // BANK
-D_PER_PART = D // P
+D_CHUNKS = D // P
 GROUP = 2
 ROUNDS = TILES // GROUP
 LOAD_TILES = 4
-VECTOR_EVERY = 6
-GPSIMD_ROUNDS = [r for r in range(2, ROUNDS) if r % 4 != 3]
-AHEAD = 4
 TAIL = 2
-LEAD = 3
 
 FLOPS = 2 * T * D * K
 BYTES = 4 * T * D + 4 * T * HALF_K + 4 * T * RANK + 2 * 2 * T * RANK + 2 * 2 * D * HALF_K
@@ -54,13 +50,10 @@ def tile_linear_pa_v_kernel(tc, x, w0, core1, core2, w1, m2, grad_out, out):
         ahead = ctx.enter_context(tc.tile_pool(name="ahead", bufs=6))
         out_pool = ctx.enter_context(tc.tile_pool(name="out", bufs=8))
         turn_psum = ctx.enter_context(tc.psum_pool(name="turn", bufs=2))
-        acc_psum = ctx.enter_context(tc.psum_pool(name="acc", bufs=5))
-        token_psum = ctx.enter_context(tc.psum_pool(name="token", bufs=1))
+        acc_psum = ctx.enter_context(tc.psum_pool(name="acc", bufs=6))
 
         ident = const.tile([P, P], F32)
         make_identity(nc, ident[:])
-        ident_bf16 = const.tile([P, P], BF16)
-        make_identity(nc, ident_bf16[:])
 
         g_sb = const.tile([P, TILES, RANK], BF16)
         w0_sb = const.tile([P, TILES, RANK], BF16)
@@ -74,56 +67,39 @@ def tile_linear_pa_v_kernel(tc, x, w0, core1, core2, w1, m2, grad_out, out):
                 m2_of[first + n] = (m2_sb, n)
 
         nc.sync.dma_start(out=g_sb[:], in_=g_dram)
-        nc.sync.dma_start(out=w1_sb[:], in_=w1_dram)
-        load_m2(0, GROUP)
         nc.sync.dma_start(out=w0_sb[:], in_=w0_dram)
-        cc_raw = const.tile([P, D_PER_PART * K], BF16)
+        load_m2(0, GROUP)
+        core_sb = []
         for h, core in enumerate((core1, core2)):
-            nc.sync.dma_start(
-                out=cc_raw[:, h * D_PER_PART * HALF_K : (h + 1) * D_PER_PART * HALF_K].rearrange(
-                    "p (a f) -> p a f", a=RANK
-                ),
-                in_=core.rearrange("a (p s) c -> p a (s c)", s=D_PER_PART),
-            )
+            raw = const.tile([P, P * RANK], BF16, name="core_%d" % h)
+            nc.sync.dma_start(out=raw[:], in_=core.rearrange("a (e l) c -> (a e) (l c)", l=P))
+            core_sb.append(raw)
+        nc.sync.dma_start(out=w1_sb[:], in_=w1_dram)
         load_m2(GROUP, LOAD_TILES - GROUP)
         for first in range(LOAD_TILES, TILES, LOAD_TILES):
             load_m2(first, LOAD_TILES)
 
         ctx.enter_context(tc.manual_schedule(engines={mybir.EngineType.PE, mybir.EngineType.DVE, mybir.EngineType.Activation, mybir.EngineType.Pool}))
-        in_psum = token_psum.tile([P, 2, TILES, RANK], BF16)
-        for slot, small in enumerate((g_sb, w0_sb)):
-            nc.tensor.matmul(
-                in_psum[:, slot].rearrange("p n r -> p (n r)"),
-                lhsT=ident_bf16[:],
-                rhs=small[:].rearrange("p n r -> p (n r)"),
-                start=True,
-                stop=True,
-            )
-
-        cc_rows = const.tile([P, D_PER_PART * K], BF16)
+        cc_rows = const.tile([P, D_CHUNKS * K], BF16)
         cc_grouped = const.tile([P, D * PACK], BF16, align_bytes=64)
         cc_codes = const.tile([P, D], U32, align_bytes=64)
         cc_scales = const.tile([P, D], U8, align_bytes=64)
 
-        def sort_cc():
-            pairs = RANK // 2
-            raw = cc_raw[:].bitcast(F32).rearrange("p (h a s c) -> p h s a c", h=2, a=RANK, c=pairs)
-            rows = cc_rows[:].bitcast(F32).rearrange("p (s h a c) -> p h s a c", h=2, a=RANK, c=pairs)
-            nc.scalar.copy(out=rows[:, 0], in_=raw[:, 0])
-            nc.vector.tensor_copy(out=rows[:, 1], in_=raw[:, 1])
+        def sort_cc(h, u, copy):
+            words = core_sb[h][:].bitcast(F32).rearrange("p (l w) -> p w l", w=RANK // 2)
+            sorted_cc = acc_psum.tile([P, BANK], F32, tag="acc")
+            for f in range(TURNS):
+                nc.tensor.transpose(sorted_cc[:, f * P : (f + 1) * P], words[:, 2 * f + u, :], ident[:])
+            rows = cc_rows[:].bitcast(F32).rearrange("p (e u h a f) -> p u h e a f", e=D_CHUNKS, u=2, h=2, a=RANK)
+            copy(out=rows[:, u, h], in_=sorted_cc[:].rearrange("p (f a e) -> p e a f", f=TURNS, a=RANK))
 
-        def turn_cc():
-            words = cc_rows[:].bitcast(F32).rearrange("p (s i u) -> p s i u", s=D_PER_PART, u=2)
-            banks = D_PER_PART * 2 // TURNS
-            grouped_words = cc_grouped[:].bitcast(F32).rearrange("p (c b f) -> p c b f", b=banks, f=TURNS)
-            for bank in range(banks):
-                turned_cc = acc_psum.tile([P, BANK], F32, tag="acc")
-                for f in range(TURNS):
-                    nc.tensor.transpose(
-                        turned_cc[:, f * P : (f + 1) * P], words[:, 2 * bank + f // 2, :, f % 2], ident[:]
-                    )
-                copy = nc.vector.tensor_copy if bank % 2 else nc.scalar.copy
-                copy(out=grouped_words[:, :, bank, :], in_=turned_cc[:].rearrange("p (f c) -> p c f", f=TURNS))
+        def turn_cc(bank, copy):
+            words = cc_rows[:].bitcast(F32).rearrange("p (e u i) -> p e u i", e=D_CHUNKS, u=2)
+            turned_cc = acc_psum.tile([P, BANK], F32, tag="acc")
+            for f in range(TURNS):
+                nc.tensor.transpose(turned_cc[:, f * P : (f + 1) * P], words[:, 2 * bank + f // 2, f % 2, :], ident[:])
+            grouped_words = cc_grouped[:].bitcast(F32).rearrange("p (b e l u) -> p b e l u", e=2, l=P, u=2)
+            copy(out=grouped_words[:, bank], in_=turned_cc[:].rearrange("p (e u l) -> p e l u", e=2, u=2))
 
         def quantise_cc(b):
             cols = slice(b * BANK, (b + 1) * BANK)
@@ -146,35 +122,24 @@ def tile_linear_pa_v_kernel(tc, x, w0, core1, core2, w1, m2, grad_out, out):
             return dm_of[rnd]
 
         def second_half(rnd):
-            dm = dm_tile(rnd)
-            for n in range(GROUP):
-                tile = rnd * GROUP + n
-                nc.gpsimd.tensor_tensor(
-                    out=dm[:, n * K + HALF_K : (n + 1) * K].rearrange("p (a c) -> p a c", a=RANK),
-                    in0=w1_sb[:, tile, :].unsqueeze(2).to_broadcast([P, RANK, RANK]),
-                    in1=g_sb[:, tile, :].unsqueeze(1).to_broadcast([P, RANK, RANK]),
-                    op=MULT,
-                )
+            tiles = slice(rnd * GROUP, (rnd + 1) * GROUP)
+            nc.vector.tensor_tensor(
+                out=dm_tile(rnd)[:].rearrange("p (n h a c) -> p h n a c", h=2, a=RANK, c=RANK)[:, 1],
+                in0=w1_sb[:, tiles, :].unsqueeze(3).to_broadcast(outer),
+                in1=g_sb[:, tiles, :].unsqueeze(2).to_broadcast(outer),
+                op=MULT,
+            )
 
         def products(rnd):
             tiles = slice(rnd * GROUP, (rnd + 1) * GROUP)
             m2_sb, first = m2_of[rnd * GROUP]
             prod = ahead.tile(outer, F32)
-            if rnd in GPSIMD_ROUNDS:
-                for n in range(GROUP):
-                    nc.gpsimd.tensor_tensor(
-                        out=prod[:, n],
-                        in0=m2_sb[:, first + n, :].rearrange("p (q r) -> p q r", r=RANK),
-                        in1=g_sb[:, rnd * GROUP + n, :].unsqueeze(1).to_broadcast([P, RANK, RANK]),
-                        op=MULT,
-                    )
-            else:
-                nc.vector.tensor_tensor(
-                    out=prod[:],
-                    in0=m2_sb[:, first : first + GROUP, :].rearrange("p n (q r) -> p n q r", r=RANK),
-                    in1=in_psum[:, 0, tiles, :].unsqueeze(2).to_broadcast(outer),
-                    op=MULT,
-                )
+            nc.vector.tensor_tensor(
+                out=prod[:],
+                in0=m2_sb[:, first : first + GROUP, :].rearrange("p n (q r) -> p n q r", r=RANK),
+                in1=g_sb[:, tiles, :].unsqueeze(2).to_broadcast(outer),
+                op=MULT,
+            )
             prod_of[rnd] = prod
 
         def sums(rnd):
@@ -186,7 +151,7 @@ def tile_linear_pa_v_kernel(tc, x, w0, core1, core2, w1, m2, grad_out, out):
             tiles = slice(rnd * GROUP, (rnd + 1) * GROUP)
             nc.vector.tensor_tensor(
                 out=dm_tile(rnd)[:].rearrange("p (n h a c) -> p h n a c", h=2, a=RANK, c=RANK)[:, 0],
-                in0=in_psum[:, 1, tiles, :].unsqueeze(3).to_broadcast(outer),
+                in0=w0_sb[:, tiles, :].unsqueeze(3).to_broadcast(outer),
                 in1=dw1_of[rnd][:].unsqueeze(2).to_broadcast(outer),
                 op=MULT,
             )
@@ -219,23 +184,22 @@ def tile_linear_pa_v_kernel(tc, x, w0, core1, core2, w1, m2, grad_out, out):
         acc_of = {}
         out_of = {}
 
-        def multiply(rnd):
+        def multiply(rnd, n):
             dm_codes, dm_scales = packed_of[rnd]
-            for n in range(GROUP):
-                tokens = slice(n * P, (n + 1) * P)
-                for b in range(D_BANKS):
-                    cols = slice(b * BANK, (b + 1) * BANK)
-                    acc = acc_psum.tile([P, BANK], F32)
-                    nc.tensor.matmul_mx(
-                        out=acc[:],
-                        lhsT=dm_codes[:, tokens].bitcast(E5M2_X4),
-                        lhsT_scale=dm_scales[:, tokens],
-                        rhs=cc_codes[:, cols].bitcast(E4M3_X4),
-                        rhs_scale=cc_scales[:, cols],
-                        start=True,
-                        stop=True,
-                    )
-                    acc_of[rnd, n, b] = acc
+            tokens = slice(n * P, (n + 1) * P)
+            for b in range(D_BANKS):
+                cols = slice(b * BANK, (b + 1) * BANK)
+                acc = acc_psum.tile([P, BANK], F32)
+                nc.tensor.matmul_mx(
+                    out=acc[:],
+                    lhsT=dm_codes[:, tokens].bitcast(E5M2_X4),
+                    lhsT_scale=dm_scales[:, tokens],
+                    rhs=cc_codes[:, cols].bitcast(E4M3_X4),
+                    rhs_scale=cc_scales[:, cols],
+                    start=True,
+                    stop=True,
+                )
+                acc_of[rnd, n, b] = acc
 
         def empty(rnd, n, b, copy):
             if b == 0:
@@ -250,38 +214,37 @@ def tile_linear_pa_v_kernel(tc, x, w0, core1, core2, w1, m2, grad_out, out):
 
         scalar, vector = nc.scalar.copy, nc.vector.tensor_copy
 
-        for rnd in range(3):
-            second_half(rnd)
         products(0)
         sums(0)
+        sort_cc(0, 0, scalar)
+        sort_cc(0, 1, scalar)
         finish_dm(0)
-        sort_cc()
+        sort_cc(1, 0, scalar)
+        sort_cc(1, 1, scalar)
+        second_half(0)
         products(1)
-        turn_cc()
         turn_dm(0)
-        group_dm(0)
+        turn_cc(0, scalar)
+        turn_cc(1, vector)
         sums(1)
+        turn_cc(2, scalar)
         quantise_cc(0)
+        turn_cc(3, vector)
+        group_dm(0)
         quantise_dm(0)
         quantise_cc(1)
-        finish_dm(1)
-        products(2)
-        second_half(3)
-        products(3)
+        second_half(1)
         for rnd in range(ROUNDS):
-            if rnd:
-                quantise_dm(rnd)
-            if rnd:
-                for_round(turn_dm, rnd + 1)
-            multiply(rnd)
-            if not rnd:
-                for_round(turn_dm, rnd + 1)
-            for_round(products, rnd + AHEAD)
-            for_round(second_half, rnd + AHEAD)
+            multiply(rnd, 0)
             empty(rnd, 0, 0, scalar)
-            for_round(group_dm, rnd + 1)
-            for_round(sums, rnd + 2)
+            for_round(finish_dm, rnd + 1)
+            for_round(turn_dm, rnd + 1)
+            multiply(rnd, 1)
             empty(rnd, 0, 1, scalar)
-            for_round(finish_dm, rnd + 2)
+            for_round(group_dm, rnd + 1)
+            for_round(products, rnd + 2)
+            for_round(second_half, rnd + 2)
+            for_round(sums, rnd + 2)
             empty(rnd, 1, 0, vector if rnd >= ROUNDS - TAIL else scalar)
-            empty(rnd, 1, 1, vector if (rnd + AHEAD >= ROUNDS or rnd + AHEAD in GPSIMD_ROUNDS) else scalar)
+            empty(rnd, 1, 1, vector if rnd >= ROUNDS - TAIL else scalar)
+            for_round(quantise_dm, rnd + 1)

@@ -27,6 +27,7 @@ D_CHUNKS = D // P
 GROUP = 2
 ROUNDS = TILES // GROUP
 LOAD_TILES = 4
+SHARED = 5
 TAIL = 2
 
 FLOPS = 2 * T * D * K
@@ -46,8 +47,8 @@ def tile_linear_pa_v_kernel(tc, x, w0, core1, core2, w1, m2, grad_out, out):
     with ExitStack() as ctx:
         const = ctx.enter_context(tc.tile_pool(name="const", bufs=1))
         short = ctx.enter_context(tc.tile_pool(name="short", bufs=2))
-        kept = ctx.enter_context(tc.tile_pool(name="kept", bufs=3))
-        ahead = ctx.enter_context(tc.tile_pool(name="ahead", bufs=6))
+        kept = ctx.enter_context(tc.tile_pool(name="kept", bufs=4))
+        ahead = ctx.enter_context(tc.tile_pool(name="ahead", bufs=8))
         out_pool = ctx.enter_context(tc.tile_pool(name="out", bufs=8))
         turn_psum = ctx.enter_context(tc.psum_pool(name="turn", bufs=2))
         acc_psum = ctx.enter_context(tc.psum_pool(name="acc", bufs=6))
@@ -66,16 +67,17 @@ def tile_linear_pa_v_kernel(tc, x, w0, core1, core2, w1, m2, grad_out, out):
             for n in range(count):
                 m2_of[first + n] = (m2_sb, n)
 
-        nc.sync.dma_start(out=g_sb[:], in_=g_dram)
-        nc.sync.dma_start(out=w0_sb[:], in_=w0_dram)
-        load_m2(0, GROUP)
         core_sb = []
         for h, core in enumerate((core1, core2)):
             raw = const.tile([P, P * RANK], BF16, name="core_%d" % h)
             nc.sync.dma_start(out=raw[:], in_=core.rearrange("a (e l) c -> (a e) (l c)", l=P))
             core_sb.append(raw)
-        nc.sync.dma_start(out=w1_sb[:], in_=w1_dram)
+            if h == 0:
+                nc.sync.dma_start(out=g_sb[:], in_=g_dram)
+                load_m2(0, GROUP)
+        nc.sync.dma_start(out=w0_sb[:], in_=w0_dram)
         load_m2(GROUP, LOAD_TILES - GROUP)
+        nc.sync.dma_start(out=w1_sb[:], in_=w1_dram)
         for first in range(LOAD_TILES, TILES, LOAD_TILES):
             load_m2(first, LOAD_TILES)
 
@@ -216,35 +218,46 @@ def tile_linear_pa_v_kernel(tc, x, w0, core1, core2, w1, m2, grad_out, out):
 
         products(0)
         sums(0)
+        finish_dm(0)
+        products(1)
+        second_half(0)
+        sums(1)
+        second_half(1)
+        finish_dm(1)
         sort_cc(0, 0, scalar)
         sort_cc(0, 1, scalar)
-        finish_dm(0)
         sort_cc(1, 0, scalar)
         sort_cc(1, 1, scalar)
-        second_half(0)
-        products(1)
-        turn_dm(0)
         turn_cc(0, scalar)
-        turn_cc(1, vector)
-        sums(1)
+        turn_cc(1, scalar)
         turn_cc(2, scalar)
-        quantise_cc(0)
-        turn_cc(3, vector)
+        turn_cc(3, scalar)
+        turn_dm(0)
         group_dm(0)
-        quantise_dm(0)
+        turn_dm(1)
+        group_dm(1)
+        products(2)
+        quantise_cc(0)
+        second_half(2)
         quantise_cc(1)
-        second_half(1)
+        quantise_dm(0)
+        sums(2)
+        products(3)
+        finish_dm(2)
         for rnd in range(ROUNDS):
             multiply(rnd, 0)
-            empty(rnd, 0, 0, scalar)
-            for_round(finish_dm, rnd + 1)
-            for_round(turn_dm, rnd + 1)
             multiply(rnd, 1)
-            empty(rnd, 0, 1, scalar)
-            for_round(group_dm, rnd + 1)
-            for_round(products, rnd + 2)
-            for_round(second_half, rnd + 2)
-            for_round(sums, rnd + 2)
-            empty(rnd, 1, 0, vector if rnd >= ROUNDS - TAIL else scalar)
-            empty(rnd, 1, 1, vector if rnd >= ROUNDS - TAIL else scalar)
+            for_round(turn_dm, rnd + 2)
+            for_round(sums, rnd + 3)
+            empty(rnd, 0, 0, scalar)
+            for_round(products, rnd + 4)
             for_round(quantise_dm, rnd + 1)
+            for_round(second_half, rnd + 3)
+            if rnd >= ROUNDS - SHARED:
+                empty(rnd, 0, 1, vector)
+            else:
+                empty(rnd, 0, 1, scalar)
+            for_round(group_dm, rnd + 2)
+            for_round(finish_dm, rnd + 3)
+            empty(rnd, 1, 0, scalar)
+            empty(rnd, 1, 1, vector if rnd >= ROUNDS - TAIL else scalar)

@@ -27,7 +27,7 @@ D_CHUNKS = D // P
 GROUP = 2
 ROUNDS = TILES // GROUP
 LOAD_TILES = 4
-SHARED = 5
+GATED = 4
 TAIL = 2
 
 FLOPS = 2 * T * D * K
@@ -50,11 +50,14 @@ def tile_linear_pa_v_kernel(tc, x, w0, core1, core2, w1, m2, grad_out, out):
         kept = ctx.enter_context(tc.tile_pool(name="kept", bufs=4))
         ahead = ctx.enter_context(tc.tile_pool(name="ahead", bufs=8))
         out_pool = ctx.enter_context(tc.tile_pool(name="out", bufs=8))
-        turn_psum = ctx.enter_context(tc.psum_pool(name="turn", bufs=2))
+        turn_psum = ctx.enter_context(tc.psum_pool(name="turn", bufs=1))
         acc_psum = ctx.enter_context(tc.psum_pool(name="acc", bufs=6))
+        token_psum = ctx.enter_context(tc.psum_pool(name="token", bufs=1))
 
         ident = const.tile([P, P], F32)
         make_identity(nc, ident[:])
+        ident_bf16 = const.tile([P, P], BF16)
+        make_identity(nc, ident_bf16[:])
 
         g_sb = const.tile([P, TILES, RANK], BF16)
         w0_sb = const.tile([P, TILES, RANK], BF16)
@@ -82,6 +85,19 @@ def tile_linear_pa_v_kernel(tc, x, w0, core1, core2, w1, m2, grad_out, out):
             load_m2(first, LOAD_TILES)
 
         ctx.enter_context(tc.manual_schedule(engines={mybir.EngineType.PE, mybir.EngineType.DVE, mybir.EngineType.Activation, mybir.EngineType.Pool}))
+        in_psum = token_psum.tile([P, 2, TILES, RANK], BF16)
+
+        def put_in_psum(slot, small):
+            nc.tensor.matmul(
+                in_psum[:, slot].rearrange("p n r -> p (n r)"),
+                lhsT=ident_bf16[:],
+                rhs=small[:].rearrange("p n r -> p (n r)"),
+                start=True,
+                stop=True,
+            )
+
+        g_f32 = const.tile([P, TILES, RANK], F32)
+
         cc_rows = const.tile([P, D_CHUNKS * K], BF16)
         cc_grouped = const.tile([P, D * PACK], BF16, align_bytes=64)
         cc_codes = const.tile([P, D], U32, align_bytes=64)
@@ -128,32 +144,36 @@ def tile_linear_pa_v_kernel(tc, x, w0, core1, core2, w1, m2, grad_out, out):
             nc.vector.tensor_tensor(
                 out=dm_tile(rnd)[:].rearrange("p (n h a c) -> p h n a c", h=2, a=RANK, c=RANK)[:, 1],
                 in0=w1_sb[:, tiles, :].unsqueeze(3).to_broadcast(outer),
-                in1=g_sb[:, tiles, :].unsqueeze(2).to_broadcast(outer),
+                in1=in_psum[:, 0, tiles, :].unsqueeze(2).to_broadcast(outer),
                 op=MULT,
             )
 
         def products(rnd):
             tiles = slice(rnd * GROUP, (rnd + 1) * GROUP)
             m2_sb, first = m2_of[rnd * GROUP]
-            prod = ahead.tile(outer, F32)
-            nc.vector.tensor_tensor(
-                out=prod[:],
-                in0=m2_sb[:, first : first + GROUP, :].rearrange("p n (q r) -> p n q r", r=RANK),
-                in1=g_sb[:, tiles, :].unsqueeze(2).to_broadcast(outer),
-                op=MULT,
-            )
+            m2_rnd = m2_sb[:, first : first + GROUP, :].rearrange("p n (q r) -> p n q r", r=RANK)
+            if rnd < GATED:
+                prod_sb = ahead.tile(outer, F32)
+                prod = prod_sb[:]
+                if rnd == 0:
+                    nc.vector.tensor_tensor(out=prod, in0=m2_rnd, in1=g_sb[:, tiles, :].unsqueeze(2).to_broadcast(outer), op=MULT)
+                else:
+                    nc.gpsimd.tensor_tensor(out=prod, in0=m2_rnd, in1=g_f32[:, tiles, :].unsqueeze(2).to_broadcast(outer), op=MULT)
+            else:
+                prod = grouped_of[rnd - 3][:].bitcast(F32).rearrange("p (n q r) -> p n q r", n=GROUP, q=RANK)
+                nc.gpsimd.tensor_tensor(out=prod, in0=m2_rnd, in1=g_f32[:, tiles, :].unsqueeze(2).to_broadcast(outer), op=MULT)
             prod_of[rnd] = prod
 
         def sums(rnd):
             dw1 = kept.tile([P, GROUP, RANK], F32)
-            nc.vector.tensor_reduce(out=dw1[:], in_=prod_of[rnd][:], axis=mybir.AxisListType.X, op=ADD)
+            nc.vector.tensor_reduce(out=dw1[:], in_=prod_of[rnd], axis=mybir.AxisListType.X, op=ADD)
             dw1_of[rnd] = dw1
 
         def finish_dm(rnd):
             tiles = slice(rnd * GROUP, (rnd + 1) * GROUP)
             nc.vector.tensor_tensor(
                 out=dm_tile(rnd)[:].rearrange("p (n h a c) -> p h n a c", h=2, a=RANK, c=RANK)[:, 0],
-                in0=w0_sb[:, tiles, :].unsqueeze(3).to_broadcast(outer),
+                in0=in_psum[:, 1, tiles, :].unsqueeze(3).to_broadcast(outer),
                 in1=dw1_of[rnd][:].unsqueeze(2).to_broadcast(outer),
                 op=MULT,
             )
@@ -217,46 +237,47 @@ def tile_linear_pa_v_kernel(tc, x, w0, core1, core2, w1, m2, grad_out, out):
         scalar, vector = nc.scalar.copy, nc.vector.tensor_copy
 
         products(0)
+        nc.vector.tensor_copy(out=g_f32[:], in_=g_sb[:])
         sums(0)
-        finish_dm(0)
         products(1)
+        products(2)
+        products(3)
+        sort_cc(0, 0, scalar)
+        sort_cc(0, 1, scalar)
+        put_in_psum(0, g_sb)
+        put_in_psum(1, w0_sb)
+        sort_cc(1, 0, scalar)
+        sort_cc(1, 1, scalar)
+        finish_dm(0)
         second_half(0)
         sums(1)
         second_half(1)
         finish_dm(1)
-        sort_cc(0, 0, scalar)
-        sort_cc(0, 1, scalar)
-        sort_cc(1, 0, scalar)
-        sort_cc(1, 1, scalar)
+        sums(2)
+        second_half(2)
         turn_cc(0, scalar)
         turn_cc(1, scalar)
-        turn_cc(2, scalar)
-        turn_cc(3, scalar)
         turn_dm(0)
         group_dm(0)
+        turn_cc(2, scalar)
+        turn_cc(3, scalar)
         turn_dm(1)
-        group_dm(1)
-        products(2)
         quantise_cc(0)
-        second_half(2)
-        quantise_cc(1)
-        quantise_dm(0)
-        sums(2)
-        products(3)
         finish_dm(2)
+        quantise_dm(0)
+        quantise_cc(1)
+        group_dm(1)
+        second_half(3)
         for rnd in range(ROUNDS):
             multiply(rnd, 0)
             multiply(rnd, 1)
             for_round(turn_dm, rnd + 2)
-            for_round(sums, rnd + 3)
             empty(rnd, 0, 0, scalar)
-            for_round(products, rnd + 4)
             for_round(quantise_dm, rnd + 1)
-            for_round(second_half, rnd + 3)
-            if rnd >= ROUNDS - SHARED:
-                empty(rnd, 0, 1, vector)
-            else:
-                empty(rnd, 0, 1, scalar)
+            for_round(products, rnd + 4)
+            for_round(sums, rnd + 3)
+            for_round(second_half, rnd + 4)
+            empty(rnd, 0, 1, vector if rnd % 2 or rnd >= ROUNDS - TAIL else scalar)
             for_round(group_dm, rnd + 2)
             for_round(finish_dm, rnd + 3)
             empty(rnd, 1, 0, scalar)

@@ -27,6 +27,7 @@ D_CHUNKS = D // P
 GROUP = 2
 ROUNDS = TILES // GROUP
 LOAD_TILES = 4
+SHARED = 5
 GATED = 4
 TAIL = 2
 
@@ -77,8 +78,8 @@ def tile_linear_pa_v_kernel(tc, x, w0, core1, core2, w1, m2, grad_out, out):
             core_sb.append(raw)
             if h == 0:
                 nc.sync.dma_start(out=g_sb[:], in_=g_dram)
+                nc.sync.dma_start(out=w0_sb[:], in_=w0_dram)
                 load_m2(0, GROUP)
-        nc.sync.dma_start(out=w0_sb[:], in_=w0_dram)
         load_m2(GROUP, LOAD_TILES - GROUP)
         nc.sync.dma_start(out=w1_sb[:], in_=w1_dram)
         for first in range(LOAD_TILES, TILES, LOAD_TILES):
@@ -237,7 +238,7 @@ def tile_linear_pa_v_kernel(tc, x, w0, core1, core2, w1, m2, grad_out, out):
         scalar, vector = nc.scalar.copy, nc.vector.tensor_copy
 
         products(0)
-        nc.vector.tensor_copy(out=g_f32[:], in_=g_sb[:])
+        nc.scalar.copy(out=g_f32[:], in_=g_sb[:])
         sums(0)
         products(1)
         products(2)
@@ -270,15 +271,15 @@ def tile_linear_pa_v_kernel(tc, x, w0, core1, core2, w1, m2, grad_out, out):
         second_half(3)
         for rnd in range(ROUNDS):
             multiply(rnd, 0)
-            multiply(rnd, 1)
             for_round(turn_dm, rnd + 2)
+            multiply(rnd, 1)
             empty(rnd, 0, 0, scalar)
             for_round(quantise_dm, rnd + 1)
             for_round(products, rnd + 4)
             for_round(sums, rnd + 3)
             for_round(second_half, rnd + 4)
-            empty(rnd, 0, 1, vector if rnd % 2 or rnd >= ROUNDS - TAIL else scalar)
+            empty(rnd, 0, 1, vector if rnd >= ROUNDS - TAIL else scalar)
             for_round(group_dm, rnd + 2)
             for_round(finish_dm, rnd + 3)
-            empty(rnd, 1, 0, scalar)
+            empty(rnd, 1, 0, vector if rnd % 3 else scalar)
             empty(rnd, 1, 1, vector if rnd >= ROUNDS - TAIL else scalar)

@@ -27,7 +27,6 @@ D_CHUNKS = D // P
 GROUP = 2
 ROUNDS = TILES // GROUP
 LOAD_TILES = 4
-SHARED = 5
 GATED = 4
 TAIL = 2
 
@@ -50,7 +49,7 @@ def tile_linear_pa_v_kernel(tc, x, w0, core1, core2, w1, m2, grad_out, out):
         short = ctx.enter_context(tc.tile_pool(name="short", bufs=2))
         kept = ctx.enter_context(tc.tile_pool(name="kept", bufs=4))
         ahead = ctx.enter_context(tc.tile_pool(name="ahead", bufs=8))
-        out_pool = ctx.enter_context(tc.tile_pool(name="out", bufs=8))
+        out_pool = ctx.enter_context(tc.tile_pool(name="out", bufs=6))
         turn_psum = ctx.enter_context(tc.psum_pool(name="turn", bufs=1))
         acc_psum = ctx.enter_context(tc.psum_pool(name="acc", bufs=6))
         token_psum = ctx.enter_context(tc.psum_pool(name="token", bufs=1))
@@ -82,8 +81,9 @@ def tile_linear_pa_v_kernel(tc, x, w0, core1, core2, w1, m2, grad_out, out):
                 load_m2(0, GROUP)
         load_m2(GROUP, LOAD_TILES - GROUP)
         nc.sync.dma_start(out=w1_sb[:], in_=w1_dram)
-        for first in range(LOAD_TILES, TILES, LOAD_TILES):
-            load_m2(first, LOAD_TILES)
+        load_m2(LOAD_TILES, LOAD_TILES)
+        for first in range(2 * LOAD_TILES, TILES, 2 * LOAD_TILES):
+            load_m2(first, 2 * LOAD_TILES)
 
         ctx.enter_context(tc.manual_schedule(engines={mybir.EngineType.PE, mybir.EngineType.DVE, mybir.EngineType.Activation, mybir.EngineType.Pool}))
         in_psum = token_psum.tile([P, 2, TILES, RANK], BF16)
@@ -225,11 +225,14 @@ def tile_linear_pa_v_kernel(tc, x, w0, core1, core2, w1, m2, grad_out, out):
                 acc_of[rnd, n, b] = acc
 
         def empty(rnd, n, b, copy):
-            if b == 0:
-                out_of[rnd, n] = out_pool.tile([P, D], F32, name="out_sb")
-            copy(out=out_of[rnd, n][:, b * BANK : (b + 1) * BANK], in_=acc_of[rnd, n, b][:])
-            if b == 1:
-                nc.sync.dma_start(out=out_dram[:, rnd * GROUP + n, :], in_=out_of[rnd, n][:])
+            if n == 0 and b == 0:
+                out_of[rnd] = out_pool.tile([P, GROUP, D], F32, name="out_sb")
+            copy(out=out_of[rnd][:, n, b * BANK : (b + 1) * BANK], in_=acc_of[rnd, n, b][:])
+            if b == D_BANKS - 1:
+                if rnd in (0, ROUNDS - 1):
+                    nc.sync.dma_start(out=out_dram[:, rnd * GROUP + n, :], in_=out_of[rnd][:, n])
+                elif n == GROUP - 1:
+                    nc.sync.dma_start(out=out_dram[:, rnd * GROUP : (rnd + 1) * GROUP, :], in_=out_of[rnd][:])
 
         def for_round(step, rnd):
             if rnd < ROUNDS:

@@ -27,8 +27,9 @@ D_CHUNKS = D // P
 GROUP = 2
 ROUNDS = TILES // GROUP
 LOAD_TILES = 4
+FIRST = 8
 GATED = 4
-TAIL = 2
+TAIL = 4
 
 FLOPS = 2 * T * D * K
 BYTES = 4 * T * D + 4 * T * HALF_K + 4 * T * RANK + 2 * 2 * T * RANK + 2 * 2 * D * HALF_K
@@ -70,18 +71,21 @@ def tile_linear_pa_v_kernel(tc, x, w0, core1, core2, w1, m2, grad_out, out):
             for n in range(count):
                 m2_of[first + n] = (m2_sb, n)
 
-        core_sb = []
-        for h, core in enumerate((core1, core2)):
-            raw = const.tile([P, P * RANK], BF16, name="core_%d" % h)
-            nc.sync.dma_start(out=raw[:], in_=core.rearrange("a (e l) c -> (a e) (l c)", l=P))
-            core_sb.append(raw)
-            if h == 0:
-                nc.sync.dma_start(out=g_sb[:], in_=g_dram)
-                nc.sync.dma_start(out=w0_sb[:], in_=w0_dram)
-                load_m2(0, GROUP)
-        load_m2(GROUP, LOAD_TILES - GROUP)
-        nc.sync.dma_start(out=w1_sb[:], in_=w1_dram)
-        load_m2(LOAD_TILES, LOAD_TILES)
+        core_sb = [const.tile([P, P * RANK], BF16, name="core_%d" % h) for h in range(2)]
+
+        def load_core(h, core):
+            nc.sync.dma_start(out=core_sb[h][:], in_=core.rearrange("a (e l) c -> (a e) (l c)", l=P))
+
+        nc.sync.dma_start(out=g_sb[:], in_=g_dram)
+        load_m2(0, GROUP)
+        load_core(0, core1)
+        nc.sync.dma_start(out=w0_sb[:], in_=w0_dram)
+        load_core(1, core2)
+        nc.sync.dma_start(out=w1_sb[:, 0:FIRST, :], in_=w1_dram[:, 0:FIRST, :])
+        load_m2(GROUP, GROUP)
+        load_m2(2 * GROUP, GROUP)
+        load_m2(3 * GROUP, GROUP)
+        nc.sync.dma_start(out=w1_sb[:, FIRST:TILES, :], in_=w1_dram[:, FIRST:TILES, :])
         for first in range(2 * LOAD_TILES, TILES, 2 * LOAD_TILES):
             load_m2(first, 2 * LOAD_TILES)
 
@@ -174,7 +178,7 @@ def tile_linear_pa_v_kernel(tc, x, w0, core1, core2, w1, m2, grad_out, out):
             tiles = slice(rnd * GROUP, (rnd + 1) * GROUP)
             nc.vector.tensor_tensor(
                 out=dm_tile(rnd)[:].rearrange("p (n h a c) -> p h n a c", h=2, a=RANK, c=RANK)[:, 0],
-                in0=in_psum[:, 1, tiles, :].unsqueeze(3).to_broadcast(outer),
+                in0=(w0_sb if rnd == 0 else in_psum[:, 1])[:, tiles, :].unsqueeze(3).to_broadcast(outer),
                 in1=dw1_of[rnd][:].unsqueeze(2).to_broadcast(outer),
                 op=MULT,
             )
@@ -240,25 +244,25 @@ def tile_linear_pa_v_kernel(tc, x, w0, core1, core2, w1, m2, grad_out, out):
 
         scalar, vector = nc.scalar.copy, nc.vector.tensor_copy
 
-        products(0)
         nc.scalar.copy(out=g_f32[:], in_=g_sb[:])
+        put_in_psum(0, g_sb)
+        products(0)
         sums(0)
         products(1)
         products(2)
         products(3)
         sort_cc(0, 0, scalar)
         sort_cc(0, 1, scalar)
-        put_in_psum(0, g_sb)
         put_in_psum(1, w0_sb)
         sort_cc(1, 0, scalar)
         sort_cc(1, 1, scalar)
         finish_dm(0)
         second_half(0)
-        sums(1)
         second_half(1)
+        sums(1)
+        second_half(2)
         finish_dm(1)
         sums(2)
-        second_half(2)
         turn_cc(0, scalar)
         turn_cc(1, scalar)
         turn_dm(0)
@@ -284,5 +288,5 @@ def tile_linear_pa_v_kernel(tc, x, w0, core1, core2, w1, m2, grad_out, out):
             empty(rnd, 0, 1, vector if rnd >= ROUNDS - TAIL else scalar)
             for_round(group_dm, rnd + 2)
             for_round(finish_dm, rnd + 3)
-            empty(rnd, 1, 0, vector if rnd % 3 else scalar)
-            empty(rnd, 1, 1, vector if rnd >= ROUNDS - TAIL else scalar)
+            empty(rnd, 1, 0, vector if rnd % 3 and rnd < ROUNDS - TAIL else scalar)
+            empty(rnd, 1, 1, vector if rnd > ROUNDS - TAIL else scalar)

from contextlib import ExitStack

import concourse.mybir as mybir
from concourse.masks import make_identity

F32 = mybir.dt.float32
BF16 = mybir.dt.bfloat16
U32 = mybir.dt.uint32
U8 = mybir.dt.uint8
E4M3_X4 = mybir.dt.float8_e4m3fn_x4
E5M2_X4 = mybir.dt.float8_e5m2_x4
MULT = mybir.AluOpType.mult
ADD = mybir.AluOpType.add

P = 128
PACK = 4
T = 4096
D = 1024
RANK = 16
HALF_K = RANK * RANK
K = 2 * HALF_K
TILES = T // P
BANK = 512
TURNS = BANK // P
D_BANKS = D // BANK
D_CHUNKS = D // P
GROUP = 2
ROUNDS = TILES // GROUP
LOAD_TILES = 4
FIRST = 8
GATED = 4
TAIL = 4

FLOPS = 2 * T * D * K
BYTES = 4 * T * D + 4 * T * HALF_K + 4 * T * RANK + 2 * 2 * T * RANK + 2 * 2 * D * HALF_K


def tile_linear_pa_v_kernel(tc, x, w0, core1, core2, w1, m2, grad_out, out):
    nc = tc.nc
    outer = [P, GROUP, RANK, RANK]

    w0_dram = w0.flatten_outer_dims().rearrange("(p n) r -> p n r", n=TILES)
    w1_dram = w1.flatten_outer_dims().rearrange("(p n) q -> p n q", n=TILES)
    g_dram = grad_out.flatten_outer_dims().rearrange("(p n) r -> p n r", n=TILES)
    m2_dram = m2.rearrange("b s q r -> (b s) (q r)").rearrange("(p n) f -> p n f", n=TILES)
    out_dram = out.flatten_outer_dims().rearrange("(p n) d -> p n d", n=TILES)

    with ExitStack() as ctx:
        const = ctx.enter_context(tc.tile_pool(name="const", bufs=1))
        short = ctx.enter_context(tc.tile_pool(name="short", bufs=2))
        kept = ctx.enter_context(tc.tile_pool(name="kept", bufs=4))
        ahead = ctx.enter_context(tc.tile_pool(name="ahead", bufs=8))
        out_pool = ctx.enter_context(tc.tile_pool(name="out", bufs=6))
        turn_psum = ctx.enter_context(tc.psum_pool(name="turn", bufs=1))
        acc_psum = ctx.enter_context(tc.psum_pool(name="acc", bufs=6))
        token_psum = ctx.enter_context(tc.psum_pool(name="token", bufs=1))

        ident = const.tile([P, P], F32)
        make_identity(nc, ident[:])
        ident_bf16 = const.tile([P, P], BF16)
        make_identity(nc, ident_bf16[:])

        g_sb = const.tile([P, TILES, RANK], BF16)
        w0_sb = const.tile([P, TILES, RANK], BF16)
        w1_sb = const.tile([P, TILES, RANK], F32)
        m2_of = {}

        def load_m2(first, count):
            m2_sb = const.tile([P, count, HALF_K], F32, name="m2_%d" % first)
            nc.sync.dma_start(out=m2_sb[:], in_=m2_dram[:, first : first + count, :])
            for n in range(count):
                m2_of[first + n] = (m2_sb, n)

        core_sb = [const.tile([P, P * RANK], BF16, name="core_%d" % h) for h in range(2)]

        def load_core(h, core):
            nc.sync.dma_start(out=core_sb[h][:], in_=core.rearrange("a (e l) c -> (a e) (l c)", l=P))

        nc.sync.dma_start(out=g_sb[:], in_=g_dram)
        load_m2(0, GROUP)
        load_core(0, core1)
        nc.sync.dma_start(out=w0_sb[:], in_=w0_dram)
        load_core(1, core2)
        nc.sync.dma_start(out=w1_sb[:, 0:FIRST, :], in_=w1_dram[:, 0:FIRST, :])
        load_m2(GROUP, GROUP)
        load_m2(2 * GROUP, GROUP)
        load_m2(3 * GROUP, GROUP)
        nc.sync.dma_start(out=w1_sb[:, FIRST:TILES, :], in_=w1_dram[:, FIRST:TILES, :])
        for first in range(2 * LOAD_TILES, TILES, 2 * LOAD_TILES):
            load_m2(first, 2 * LOAD_TILES)

        ctx.enter_context(tc.manual_schedule(engines={mybir.EngineType.PE, mybir.EngineType.DVE, mybir.EngineType.Activation, mybir.EngineType.Pool}))
        in_psum = token_psum.tile([P, 2, TILES, RANK], BF16)

        def put_in_psum(slot, small):
            nc.tensor.matmul(
                in_psum[:, slot].rearrange("p n r -> p (n r)"),
                lhsT=ident_bf16[:],
                rhs=small[:].rearrange("p n r -> p (n r)"),
                start=True,
                stop=True,
            )

        g_f32 = const.tile([P, TILES, RANK], F32)

        cc_rows = const.tile([P, D_CHUNKS * K], BF16)
        cc_grouped = const.tile([P, D * PACK], BF16, align_bytes=64)
        cc_codes = const.tile([P, D], U32, align_bytes=64)
        cc_scales = const.tile([P, D], U8, align_bytes=64)

        def sort_cc(h, u, copy):
            words = core_sb[h][:].bitcast(F32).rearrange("p (l w) -> p w l", w=RANK // 2)
            sorted_cc = acc_psum.tile([P, BANK], F32, tag="acc")
            for f in range(TURNS):
                nc.tensor.transpose(sorted_cc[:, f * P : (f + 1) * P], words[:, 2 * f + u, :], ident[:])
            rows = cc_rows[:].bitcast(F32).rearrange("p (e u h a f) -> p u h e a f", e=D_CHUNKS, u=2, h=2, a=RANK)
            copy(out=rows[:, u, h], in_=sorted_cc[:].rearrange("p (f a e) -> p e a f", f=TURNS, a=RANK))

        def turn_cc(bank, copy):
            words = cc_rows[:].bitcast(F32).rearrange("p (e u i) -> p e u i", e=D_CHUNKS, u=2)
            turned_cc = acc_psum.tile([P, BANK], F32, tag="acc")
            for f in range(TURNS):
                nc.tensor.transpose(turned_cc[:, f * P : (f + 1) * P], words[:, 2 * bank + f // 2, f % 2, :], ident[:])
            grouped_words = cc_grouped[:].bitcast(F32).rearrange("p (b e l u) -> p b e l u", e=2, l=P, u=2)
            copy(out=grouped_words[:, bank], in_=turned_cc[:].rearrange("p (e u l) -> p e l u", e=2, u=2))

        def quantise_cc(b):
            cols = slice(b * BANK, (b + 1) * BANK)
            nc.vector.quantize_mx(
                out=cc_codes[:, cols].bitcast(E4M3_X4),
                scales=cc_scales[:, cols],
                in_=cc_grouped[:, b * BANK * PACK : (b + 1) * BANK * PACK],
            )

        dm_of = {}
        dw1_of = {}
        grouped_of = {}
        packed_of = {}

        prod_of = {}

        def dm_tile(rnd):
            if rnd not in dm_of:
                dm_of[rnd] = ahead.tile([P, GROUP * K], BF16, name="dm")
            return dm_of[rnd]

        def second_half(rnd):
            tiles = slice(rnd * GROUP, (rnd + 1) * GROUP)
            nc.vector.tensor_tensor(
                out=dm_tile(rnd)[:].rearrange("p (n h a c) -> p h n a c", h=2, a=RANK, c=RANK)[:, 1],
                in0=w1_sb[:, tiles, :].unsqueeze(3).to_broadcast(outer),
                in1=in_psum[:, 0, tiles, :].unsqueeze(2).to_broadcast(outer),
                op=MULT,
            )

        def products(rnd):
            tiles = slice(rnd * GROUP, (rnd + 1) * GROUP)
            m2_sb, first = m2_of[rnd * GROUP]
            m2_rnd = m2_sb[:, first : first + GROUP, :].rearrange("p n (q r) -> p n q r", r=RANK)
            if rnd < GATED:
                prod_sb = ahead.tile(outer, F32)
                prod = prod_sb[:]
                if rnd == 0:
                    nc.vector.tensor_tensor(out=prod, in0=m2_rnd, in1=g_sb[:, tiles, :].unsqueeze(2).to_broadcast(outer), op=MULT)
                else:
                    nc.gpsimd.tensor_tensor(out=prod, in0=m2_rnd, in1=g_f32[:, tiles, :].unsqueeze(2).to_broadcast(outer), op=MULT)
            else:
                prod = grouped_of[rnd - 3][:].bitcast(F32).rearrange("p (n q r) -> p n q r", n=GROUP, q=RANK)
                nc.gpsimd.tensor_tensor(out=prod, in0=m2_rnd, in1=g_f32[:, tiles, :].unsqueeze(2).to_broadcast(outer), op=MULT)
            prod_of[rnd] = prod

        def sums(rnd):
            dw1 = kept.tile([P, GROUP, RANK], F32)
            nc.vector.tensor_reduce(out=dw1[:], in_=prod_of[rnd], axis=mybir.AxisListType.X, op=ADD)
            dw1_of[rnd] = dw1

        def finish_dm(rnd):
            tiles = slice(rnd * GROUP, (rnd + 1) * GROUP)
            nc.vector.tensor_tensor(
                out=dm_tile(rnd)[:].rearrange("p (n h a c) -> p h n a c", h=2, a=RANK, c=RANK)[:, 0],
                in0=(w0_sb if rnd == 0 else in_psum[:, 1])[:, tiles, :].unsqueeze(3).to_broadcast(outer),
                in1=dw1_of[rnd][:].unsqueeze(2).to_broadcast(outer),
                op=MULT,
            )

        turned_of = {}

        def turn_dm(rnd):
            words = dm_of[rnd][:].bitcast(F32).rearrange("p (n i u) -> p n i u", n=GROUP, u=2)
            turned = turn_psum.tile([P, BANK], F32)
            for f in range(TURNS):
                nc.tensor.transpose(turned[:, f * P : (f + 1) * P], words[:, f // 2, :, f % 2], ident[:])
            turned_of[rnd] = turned

        def group_dm(rnd):
            grouped = kept.tile([P, GROUP * P * PACK], BF16, align_bytes=64)
            nc.scalar.copy(
                out=grouped[:].bitcast(F32).rearrange("p (n c u) -> p n c u", n=GROUP, u=2),
                in_=turned_of[rnd][:].rearrange("p (n u c) -> p n c u", n=GROUP, u=2),
            )
            grouped_of[rnd] = grouped

        def quantise_dm(rnd):
            dm_codes = kept.tile([P, GROUP * P], U32, align_bytes=64)
            dm_scales = kept.tile([P, GROUP * P], U8, align_bytes=64)
            nc.vector.quantize_mx(
                out=dm_codes[:].bitcast(E5M2_X4), scales=dm_scales[:], in_=grouped_of[rnd][:]
            )
            packed_of[rnd] = (dm_codes, dm_scales)

        acc_of = {}
        out_of = {}

        def multiply(rnd, n):
            dm_codes, dm_scales = packed_of[rnd]
            tokens = slice(n * P, (n + 1) * P)
            for b in range(D_BANKS):
                cols = slice(b * BANK, (b + 1) * BANK)
                acc = acc_psum.tile([P, BANK], F32)
                nc.tensor.matmul_mx(
                    out=acc[:],
                    lhsT=dm_codes[:, tokens].bitcast(E5M2_X4),
                    lhsT_scale=dm_scales[:, tokens],
                    rhs=cc_codes[:, cols].bitcast(E4M3_X4),
                    rhs_scale=cc_scales[:, cols],
                    start=True,
                    stop=True,
                )
                acc_of[rnd, n, b] = acc

        def empty(rnd, n, b, copy):
            if n == 0 and b == 0:
                out_of[rnd] = out_pool.tile([P, GROUP, D], F32, name="out_sb")
            copy(out=out_of[rnd][:, n, b * BANK : (b + 1) * BANK], in_=acc_of[rnd, n, b][:])
            if b == D_BANKS - 1:
                if rnd in (0, ROUNDS - 1):
                    nc.sync.dma_start(out=out_dram[:, rnd * GROUP + n, :], in_=out_of[rnd][:, n])
                elif n == GROUP - 1:
                    nc.sync.dma_start(out=out_dram[:, rnd * GROUP : (rnd + 1) * GROUP, :], in_=out_of[rnd][:])

        def for_round(step, rnd):
            if rnd < ROUNDS:
                step(rnd)

        scalar, vector = nc.scalar.copy, nc.vector.tensor_copy

        nc.scalar.copy(out=g_f32[:], in_=g_sb[:])
        put_in_psum(0, g_sb)
        products(0)
        sums(0)
        products(1)
        products(2)
        products(3)
        sort_cc(0, 0, scalar)
        sort_cc(0, 1, scalar)
        put_in_psum(1, w0_sb)
        sort_cc(1, 0, scalar)
        sort_cc(1, 1, scalar)
        finish_dm(0)
        second_half(0)
        second_half(1)
        sums(1)
        second_half(2)
        finish_dm(1)
        sums(2)
        turn_cc(0, scalar)
        turn_cc(1, scalar)
        turn_dm(0)
        group_dm(0)
        turn_cc(2, scalar)
        turn_cc(3, scalar)
        turn_dm(1)
        quantise_cc(0)
        finish_dm(2)
        quantise_dm(0)
        quantise_cc(1)
        group_dm(1)
        second_half(3)
        for rnd in range(ROUNDS):
            multiply(rnd, 0)
            for_round(turn_dm, rnd + 2)
            multiply(rnd, 1)
            empty(rnd, 0, 0, scalar)
            for_round(quantise_dm, rnd + 1)
            for_round(products, rnd + 4)
            for_round(sums, rnd + 3)
            for_round(second_half, rnd + 4)
            empty(rnd, 0, 1, vector if rnd >= ROUNDS - TAIL else scalar)
            for_round(group_dm, rnd + 2)
            for_round(finish_dm, rnd + 3)
            empty(rnd, 1, 0, vector if rnd % 3 and rnd < ROUNDS - TAIL else scalar)
            empty(rnd, 1, 1, vector if rnd > ROUNDS - TAIL else scalar)
